import numpy as np
import ml_dtypes


def mxq(x, axis, fmt="e4m3"):
    dtype, down = {"e4m3": (ml_dtypes.float8_e4m3fn, 7), "e5m2": (ml_dtypes.float8_e5m2, 14)}[fmt]
    v = np.moveaxis(np.asarray(x, np.float32).astype(ml_dtypes.bfloat16).astype(np.float64), axis, -1)
    blocks = v.reshape(v.shape[:-1] + (-1, 32))
    amax = np.abs(blocks).max(-1, keepdims=True)
    byte = np.maximum(np.where(amax > 0, np.frexp(amax)[1] - 1 + 127, 0) - down, 1)
    scale = np.exp2(byte - 127.0)
    codes = (blocks / scale).astype(np.float32).astype(dtype).astype(np.float64)
    return np.moveaxis((codes * scale).reshape(v.shape), -1, axis)


WIDE = False


def mx_kscale(k):
    if not WIDE:
        return np.ones(k)
    levels = np.array([10, -10, 5, -5, 0])
    a = np.random.permutation(np.resize(levels, k // 512 * 4)).reshape(k // 512, 4)
    idx = np.arange(k)
    return np.exp2(a[idx // 512, idx % 128 // 32])


BF16 = ml_dtypes.bfloat16


def bf(x):
    return np.asarray(x, np.float32).astype(BF16)


def f64(x):
    return np.asarray(x).astype(np.float64)


E2M1 = np.array([0.0, 0.5, 1.0, 1.5, 2.0, 3.0, 4.0, 6.0, -0.0, -0.5, -1.0, -1.5, -2.0, -3.0, -4.0, -6.0])


def pack_weight(w, fmt):
    k, n = w.shape
    w = f64(bf(w)).reshape(k // 32, 32, n)
    amax = np.abs(w).max(1)
    if fmt == "e4m3":
        byte = np.frexp(amax)[1] - 1 + 127 - 7
    else:
        mant, ex = np.frexp(amax / 6.0)
        byte = np.where(mant > 0.5, ex, ex - 1) + 127
    byte = np.clip(np.where(amax > 0, byte, 1), 1, 254)
    scaled = (w * np.exp2(127.0 - byte)[:, None, :]).reshape(k, n).astype(np.float32)
    by_word = np.ascontiguousarray(scaled.reshape(k // 512, 128, 4, n).transpose(0, 1, 3, 2))
    if fmt == "e4m3":
        words = by_word.astype(ml_dtypes.float8_e4m3fn).view(np.uint8)
    else:
        c = by_word.astype(ml_dtypes.float4_e2m1fn).view(np.uint8) & 0xF
        words = c[..., 0::2] | (c[..., 1::2] << 4)
    return np.ascontiguousarray(words), np.ascontiguousarray(byte.astype(np.uint8).reshape(k // 512, 16, n))


def unpack_weight(words, scales, fmt):
    g, p, n, _ = words.shape
    if fmt == "e4m3":
        vals = np.ascontiguousarray(words).view(ml_dtypes.float8_e4m3fn).astype(np.float64)
    else:
        nib = np.empty((g, p, n, 4), np.uint8)
        nib[..., 0::2] = words & 0xF
        nib[..., 1::2] = words >> 4
        vals = E2M1[nib]
    vals = vals * np.repeat(np.exp2(scales.astype(np.float64) - 127.0), 8, axis=1)[..., None]
    return vals.transpose(0, 1, 3, 2).reshape(g * 512, n)


B, I, H = 128, 2048, 1536
EPS = 1e-12
FORGET_BIAS = 1.0


def layer_norm(x, g, b):
    mean = np.mean(x, axis=-1, keepdims=True)
    var = np.mean((x - mean) ** 2, axis=-1, keepdims=True)
    var_filter = 0.01 * (var < EPS).astype(np.float64)
    normalized = (x - mean) / np.sqrt(var + EPS + var_filter)
    return g * normalized + b


def sigmoid(v):
    return 1.0 / (1.0 + np.exp(-v))


def setup_inputs():
    s, t = mx_kscale(I), mx_kscale(H)
    x = bf(np.random.standard_normal((B, I)) * s)
    hx = bf(np.random.standard_normal((B, H)) * t)
    cx = bf(np.random.standard_normal((B, H)))
    weight_ih = np.random.standard_normal((4 * H, I)) / np.sqrt(I) / s[None, :]
    weight_hh = np.random.standard_normal((4 * H, H)) / np.sqrt(H) / t[None, :]
    gamma = bf(1.0 + 0.1 * np.random.standard_normal((5, H)))
    beta = bf(0.1 * np.random.standard_normal((5, H)))
    ih_words, ih_scales = pack_weight(np.ascontiguousarray(weight_ih.T), "e4m3")
    hh_words, hh_scales = pack_weight(np.ascontiguousarray(weight_hh.T), "e4m3")
    return {"x": x,
            "hx": hx,
            "cx": cx,
            "weight_ih_words": ih_words,
            "weight_ih_scales": ih_scales,
            "weight_hh_words": hh_words,
            "weight_hh_scales": hh_scales,
            "gamma": gamma,
            "beta": beta}


def reference(x, hx, cx, weight_ih_words, weight_ih_scales, weight_hh_words, weight_hh_scales, gamma, beta):
    cx, gamma, beta = f64(cx), f64(gamma), f64(beta)
    gates = (mxq(f64(x), 1, "e4m3") @ unpack_weight(weight_ih_words, weight_ih_scales, "e4m3")) + (mxq(f64(hx), 1, "e4m3") @ unpack_weight(weight_hh_words, weight_hh_scales, "e4m3"))
    ingate, forgetgate, cellgate, outgate = np.split(gates, 4, axis=1)
    ingate = layer_norm(ingate, gamma[0], beta[0])
    forgetgate = layer_norm(forgetgate, gamma[1], beta[1])
    cellgate = layer_norm(cellgate, gamma[2], beta[2])
    outgate = layer_norm(outgate, gamma[3], beta[3])
    ingate = sigmoid(ingate)
    forgetgate = sigmoid(forgetgate + FORGET_BIAS)
    cellgate = np.tanh(cellgate)
    outgate = sigmoid(outgate)
    cy = forgetgate * cx + ingate * cellgate
    cy = layer_norm(cy, gamma[4], beta[4])
    hy = outgate * np.tanh(cy)
    hy_dropped = hy
    return (hy_dropped, hy, cy)

@@ -1,0 +1,217 @@
+import concourse.mybir as mybir
+from concourse.masks import make_identity
+
+F32 = mybir.dt.float32
+BF16 = mybir.dt.bfloat16
+I32 = mybir.dt.int32
+U8 = mybir.dt.uint8
+U32 = mybir.dt.uint32
+FP8X4 = mybir.dt.float8_e4m3fn_x4
+ALU = mybir.AluOpType
+ACT = mybir.ActivationFunctionType
+
+P = 128
+IN = 2048
+H = 1536
+PASSES_X = 4
+PASSES = 7
+NB = 512
+CH = 3
+EPS = 1e-12
+FLOPS = 2 * 128 * (2048 + 1536) * 4 * 1536
+
+
+def tile_layernormdropoutlstmcell_w_kernel(
+    tc, x, hx, cx, wih_w, wih_s, whh_w, whh_s, gamma, beta, out_0, out_1, out_2
+):
+    nc = tc.nc
+    with tc.tile_pool(name="keep", bufs=1) as keep, tc.tile_pool(name="wpool", bufs=20) as wpool, tc.tile_pool(
+        name="work", bufs=1
+    ) as work, tc.tile_pool(name="small", bufs=3) as small, tc.psum_pool(name="accp", bufs=2) as accp, tc.psum_pool(
+        name="aux", bufs=2
+    ) as aux:
+        planes_ih = keep.tile([P, 4 * H], U8, align_bytes=64)
+        planes_hh = keep.tile([P, 4 * H], U8, align_bytes=64)
+        gb = keep.tile([P, H], BF16)
+        nc.vector.memset(planes_ih[:].bitcast(I32), 0)
+        nc.vector.memset(planes_hh[:].bitcast(I32), 0)
+        nc.vector.memset(gb[:].bitcast(I32), 0)
+        neg_half = keep.tile([P, 1], F32)
+        nc.vector.memset(neg_half[:], -0.5)
+        ident_f = keep.tile([P, P], F32)
+        make_identity(nc, ident_f[:])
+        ident_b = keep.tile([P, P], BF16)
+        make_identity(nc, ident_b[:])
+
+        x_sb = keep.tile([P, IN], BF16)
+        hx_sb = keep.tile([P, H], BF16)
+        cx_sb = keep.tile([P, H], BF16)
+        nc.sync.dma_start(out=x_sb[:], in_=x)
+        nc.sync.dma_start(out=hx_sb[:], in_=hx)
+        nc.scalar.dma_start(out=gb[0:10:2, :], in_=gamma)
+        nc.scalar.dma_start(out=gb[1:10:2, :], in_=beta)
+        nc.scalar.dma_start(out=cx_sb[:], in_=cx)
+        for q in (0, 2, 1, 3):
+            nc.sync.dma_start(
+                out=planes_ih[32 * q : 32 * q + 16, :].bitcast(I32), in_=wih_s[:, 4 * q : 4 * q + 4, :].bitcast(I32)
+            )
+            nc.sync.dma_start(
+                out=planes_hh[32 * q : 32 * q + 12, :].bitcast(I32), in_=whh_s[:, 4 * q : 4 * q + 4, :].bitcast(I32)
+            )
+
+        def load_gate(gate):
+            tiles = []
+            for c in range(PASSES):
+                w = wpool.tile([P, 4 * H], U8, tag="w", align_bytes=64)
+                src = wih_w[c] if c < PASSES_X else whh_w[c - PASSES_X]
+                src = src.rearrange("p n t -> p (n t)")[:, gate * 4 * H : (gate + 1) * 4 * H]
+                nc.sync.dma_start(out=w[:].bitcast(I32), in_=src.bitcast(I32))
+                tiles.append(w)
+            return tiles
+
+        w_i = load_gate(0)
+        w_f = load_gate(1)
+
+        grouped = keep.tile([P, PASSES * NB], BF16, align_bytes=64)
+        codes = keep.tile([P, PASSES * P], U32, align_bytes=64)
+        xs = keep.tile([P, PASSES * P], U8, align_bytes=64)
+        grouped_w = grouped[:].bitcast(F32).rearrange("p (c b u) -> p c b u", b=P, u=2)
+        xw = x_sb[:].bitcast(F32)
+        hw = hx_sb[:].bitcast(F32)
+        for h in range(4):
+            n_c = 2 if h < 3 else 1
+            xt = aux.tile([P, NB], F32, tag="aux")
+            for j in range(n_c):
+                c = 2 * h + j
+                src = xw if c < PASSES_X else hw
+                c0 = c if c < PASSES_X else c - PASSES_X
+                for u in range(2):
+                    nc.tensor.transpose(
+                        xt[:, (2 * j + u) * P : (2 * j + u + 1) * P],
+                        src[:, 256 * c0 + u : 256 * (c0 + 1) : 2],
+                        ident_f[:],
+                    )
+            nc.vector.tensor_copy(
+                out=grouped_w[:, 2 * h : 2 * h + n_c, :, :],
+                in_=xt[:, 0 : n_c * 256].rearrange("p (c u b) -> p c b u", u=2, b=P),
+            )
+        for lo, n in ((0, 2048), (2048, 1024), (3072, 512)):
+            nc.vector.quantize_mx(
+                out=codes[:, lo // 4 : (lo + n) // 4].bitcast(FP8X4),
+                scales=xs[:, lo // 4 : (lo + n) // 4],
+                in_=grouped[:, lo : lo + n],
+            )
+
+        gbb = keep.tile([P, 10 * H], BF16)
+        for t in range(15):
+            bc = aux.tile([P, 2 * NB], BF16, tag="aux")
+            for e in range(2):
+                piece = 2 * t + e
+                row, s = piece // CH, piece % CH
+                nc.tensor.matmul(
+                    out=bc[:, e * NB : (e + 1) * NB],
+                    lhsT=ident_b[:, row : row + 1].to_broadcast([P, P]),
+                    rhs=gb[:, s * NB : (s + 1) * NB],
+                    start=True,
+                    stop=True,
+                )
+            nc.scalar.copy(out=gbb[:, t * 2 * NB : (t + 1) * 2 * NB], in_=bc[:])
+
+        def gam(k, s):
+            return gbb[:, 2 * k * H + s * NB : 2 * k * H + (s + 1) * NB]
+
+        def bet(k, s):
+            return gbb[:, (2 * k + 1) * H + s * NB : (2 * k + 1) * H + (s + 1) * NB]
+
+        def cols(s):
+            return slice(s * NB, (s + 1) * NB)
+
+        def gate_passes(gate, tiles):
+            acc = [accp.tile([P, NB], F32, name="acc%d" % s, tag="acc%d" % s) for s in range(CH)]
+            for c in range(PASSES):
+                plane = planes_ih if c < PASSES_X else planes_hh
+                k = 4 * c if c < PASSES_X else 4 * (c - PASSES_X)
+                for s in range(CH):
+                    col0 = gate * H + s * NB
+                    nc.tensor.matmul_mx(
+                        out=acc[s][:],
+                        lhsT=codes[:, P * c : P * (c + 1)].bitcast(FP8X4),
+                        lhsT_scale=xs[:, P * c : P * (c + 1)],
+                        rhs=tiles[c][:, 4 * NB * s : 4 * NB * (s + 1)].bitcast(FP8X4),
+                        rhs_scale=plane[k:P, col0 : col0 + NB],
+                        start=(c == 0),
+                        stop=(c == PASSES - 1),
+                    )
+            return [a[:] for a in acc]
+
+        def ln_stats(chunks):
+            stats = small.tile([P, 6 * CH], F32, tag="stats")
+            for s in range(CH):
+                nc.vector.bn_stats(out=stats[:, 6 * s : 6 * s + 6], in_=chunks[s])
+            mv = small.tile([P, 2], F32, tag="mv")
+            nc.vector.bn_aggr(out=mv[:], in_=stats[:])
+            flt = small.tile([P, 1], F32, tag="flt")
+            nc.vector.tensor_scalar(
+                out=flt[:], in0=mv[:, 1:2], scalar1=EPS, scalar2=0.01, op0=ALU.is_lt, op1=ALU.mult
+            )
+            veps = small.tile([P, 1], F32, tag="veps")
+            nc.vector.scalar_tensor_tensor(
+                out=veps[:], in0=mv[:, 1:2], scalar=EPS, in1=flt[:], op0=ALU.add, op1=ALU.add
+            )
+            rstd = small.tile([P, 1], F32, tag="rstd")
+            nc.gpsimd.tensor_tensor(out=rstd[:], in0=veps[:], in1=neg_half[:], op=ALU.pow)
+            return mv[:, 0:1], rstd[:]
+
+        def ln_apply(dst, chunks, k, mean, rstd, s):
+            nc.vector.scalar_tensor_tensor(
+                out=dst[:, cols(s)], in0=chunks[s], scalar=mean, in1=gam(k, s), op0=ALU.subtract, op1=ALU.mult
+            )
+            nc.vector.scalar_tensor_tensor(
+                out=dst[:, cols(s)], in0=dst[:, cols(s)], scalar=rstd, in1=bet(k, s), op0=ALU.mult, op1=ALU.add
+            )
+
+        g_i = work.tile([P, H], F32)
+        g_f = work.tile([P, H], F32)
+        g_g = work.tile([P, H], F32)
+        g_o = work.tile([P, H], F32)
+        cy = work.tile([P, H], F32)
+        th = work.tile([P, H], F32)
+
+        acc_i = gate_passes(0, w_i)
+        w_g = load_gate(2)
+        mean, rstd = ln_stats(acc_i)
+        for s in range(CH):
+            ln_apply(g_i, acc_i, 0, mean, rstd, s)
+            nc.scalar.activation(out=g_i[:, cols(s)], in_=g_i[:, cols(s)], func=ACT.Sigmoid)
+
+        acc_f = gate_passes(1, w_f)
+        w_o = load_gate(3)
+        mean, rstd = ln_stats(acc_f)
+        for s in range(CH):
+            ln_apply(g_f, acc_f, 1, mean, rstd, s)
+            nc.scalar.activation(out=g_f[:, cols(s)], in_=g_f[:, cols(s)], func=ACT.Sigmoid, bias=1.0)
+            nc.vector.tensor_tensor(out=g_f[:, cols(s)], in0=g_f[:, cols(s)], in1=cx_sb[:, cols(s)], op=ALU.mult)
+
+        acc_g = gate_passes(2, w_g)
+        mean, rstd = ln_stats(acc_g)
+        for s in range(CH):
+            ln_apply(g_g, acc_g, 2, mean, rstd, s)
+            nc.scalar.activation(out=g_g[:, cols(s)], in_=g_g[:, cols(s)], func=ACT.Tanh)
+            nc.vector.tensor_tensor(out=g_g[:, cols(s)], in0=g_g[:, cols(s)], in1=g_i[:, cols(s)], op=ALU.mult)
+            nc.vector.tensor_tensor(out=g_g[:, cols(s)], in0=g_g[:, cols(s)], in1=g_f[:, cols(s)], op=ALU.add)
+
+        c_chunks = [g_g[:, cols(s)] for s in range(CH)]
+        mean, rstd = ln_stats(c_chunks)
+        for s in range(CH):
+            ln_apply(cy, c_chunks, 4, mean, rstd, s)
+            nc.scalar.activation(out=th[:, cols(s)], in_=cy[:, cols(s)], func=ACT.Tanh)
+        nc.sync.dma_start(out=out_2, in_=cy[:])
+
+        acc_o = gate_passes(3, w_o)
+        mean, rstd = ln_stats(acc_o)
+        for s in range(CH):
+            ln_apply(g_o, acc_o, 3, mean, rstd, s)
+            nc.scalar.activation(out=g_o[:, cols(s)], in_=g_o[:, cols(s)], func=ACT.Sigmoid)
+            nc.vector.tensor_tensor(out=g_o[:, cols(s)], in0=g_o[:, cols(s)], in1=th[:, cols(s)], op=ALU.mult)
+            nc.sync.dma_start(out=out_0[:, cols(s)], in_=g_o[:, cols(s)])
+            nc.sync.dma_start(out=out_1[:, cols(s)], in_=g_o[:, cols(s)])

@@ -48,16 +48,16 @@ def tile_layernormdropoutlstmcell_w_kernel(
         cx_sb = keep.tile([P, H], BF16)
         nc.sync.dma_start(out=x_sb[:], in_=x)
         nc.sync.dma_start(out=hx_sb[:], in_=hx)
+        for q in (0, 2, 1, 3):
+            nc.scalar.dma_start(
+                out=planes_ih[32 * q : 32 * q + 16, :].bitcast(F32), in_=wih_s[:, 4 * q : 4 * q + 4, :].bitcast(F32)
+            )
+            nc.scalar.dma_start(
+                out=planes_hh[32 * q : 32 * q + 12, :].bitcast(F32), in_=whh_s[:, 4 * q : 4 * q + 4, :].bitcast(F32)
+            )
         nc.scalar.dma_start(out=gb[0:10:2, :], in_=gamma)
         nc.scalar.dma_start(out=gb[1:10:2, :], in_=beta)
         nc.scalar.dma_start(out=cx_sb[:], in_=cx)
-        for q in (0, 2, 1, 3):
-            nc.sync.dma_start(
-                out=planes_ih[32 * q : 32 * q + 16, :].bitcast(I32), in_=wih_s[:, 4 * q : 4 * q + 4, :].bitcast(I32)
-            )
-            nc.sync.dma_start(
-                out=planes_hh[32 * q : 32 * q + 12, :].bitcast(I32), in_=whh_s[:, 4 * q : 4 * q + 4, :].bitcast(I32)
-            )
 
         def load_gate(gate):
             tiles = []

@@ -1,3 +1,5 @@
+from contextlib import ExitStack
+
 import concourse.mybir as mybir
 from concourse.masks import make_identity
 
@@ -25,17 +27,21 @@ def tile_layernormdropoutlstmcell_w_kernel(
     tc, x, hx, cx, wih_w, wih_s, whh_w, whh_s, gamma, beta, out_0, out_1, out_2
 ):
     nc = tc.nc
-    with tc.tile_pool(name="keep", bufs=1) as keep, tc.tile_pool(name="wpool", bufs=20) as wpool, tc.tile_pool(
-        name="work", bufs=1
-    ) as work, tc.tile_pool(name="small", bufs=3) as small, tc.psum_pool(name="accp", bufs=2) as accp, tc.psum_pool(
-        name="aux", bufs=2
-    ) as aux:
+    with ExitStack() as stack:
+        keep = stack.enter_context(tc.tile_pool(name="keep", bufs=1))
+        wpool = stack.enter_context(tc.tile_pool(name="wpool", bufs=18))
+        wlast = stack.enter_context(tc.tile_pool(name="wlast", bufs=6))
+        work = stack.enter_context(tc.tile_pool(name="work", bufs=1))
+        small = stack.enter_context(tc.tile_pool(name="small", bufs=3))
+        accp = stack.enter_context(tc.psum_pool(name="accp", bufs=2))
+        aux = stack.enter_context(tc.psum_pool(name="aux", bufs=2))
+
         planes_ih = keep.tile([P, 4 * H], U8, align_bytes=64)
         planes_hh = keep.tile([P, 4 * H], U8, align_bytes=64)
         gb = keep.tile([P, H], BF16)
+        nc.vector.memset(gb[:].bitcast(I32), 0)
         nc.vector.memset(planes_ih[:].bitcast(I32), 0)
         nc.vector.memset(planes_hh[:].bitcast(I32), 0)
-        nc.vector.memset(gb[:].bitcast(I32), 0)
         neg_half = keep.tile([P, 1], F32)
         nc.vector.memset(neg_half[:], -0.5)
         ident_f = keep.tile([P, P], F32)
@@ -48,29 +54,44 @@ def tile_layernormdropoutlstmcell_w_kernel(
         cx_sb = keep.tile([P, H], BF16)
         nc.sync.dma_start(out=x_sb[:], in_=x)
         nc.sync.dma_start(out=hx_sb[:], in_=hx)
-        for q in (0, 2, 1, 3):
-            nc.scalar.dma_start(
-                out=planes_ih[32 * q : 32 * q + 16, :].bitcast(F32), in_=wih_s[:, 4 * q : 4 * q + 4, :].bitcast(F32)
-            )
-            nc.scalar.dma_start(
-                out=planes_hh[32 * q : 32 * q + 12, :].bitcast(F32), in_=whh_s[:, 4 * q : 4 * q + 4, :].bitcast(F32)
-            )
         nc.scalar.dma_start(out=gb[0:10:2, :], in_=gamma)
         nc.scalar.dma_start(out=gb[1:10:2, :], in_=beta)
         nc.scalar.dma_start(out=cx_sb[:], in_=cx)
 
-        def load_gate(gate):
+        def load_scales(lo, hi):
+            for q in (0, 2, 1, 3):
+                nc.sync.dma_start(
+                    out=planes_ih[32 * q : 32 * q + 16, lo:hi].bitcast(I32),
+                    in_=wih_s[:, 4 * q : 4 * q + 4, lo:hi].bitcast(I32),
+                )
+                nc.sync.dma_start(
+                    out=planes_hh[32 * q : 32 * q + 12, lo:hi].bitcast(I32),
+                    in_=whh_s[:, 4 * q : 4 * q + 4, lo:hi].bitcast(I32),
+                )
+
+        def load_gate(gate, split_last):
             tiles = []
             for c in range(PASSES):
-                w = wpool.tile([P, 4 * H], U8, tag="w", align_bytes=64)
                 src = wih_w[c] if c < PASSES_X else whh_w[c - PASSES_X]
                 src = src.rearrange("p n t -> p (n t)")[:, gate * 4 * H : (gate + 1) * 4 * H]
-                nc.sync.dma_start(out=w[:].bitcast(I32), in_=src.bitcast(I32))
-                tiles.append(w)
+                if split_last and c == PASSES - 1:
+                    pieces = []
+                    for s in range(CH):
+                        wl = wlast.tile([P, 4 * NB], U8, tag="wl", align_bytes=64)
+                        nc.sync.dma_start(out=wl[:].bitcast(I32), in_=src[:, 4 * NB * s : 4 * NB * (s + 1)].bitcast(I32))
+                        pieces.append(wl[:])
+                    tiles.append(pieces)
+                else:
+                    w = wpool.tile([P, 4 * H], U8, tag="w", align_bytes=64)
+                    nc.sync.dma_start(out=w[:].bitcast(I32), in_=src.bitcast(I32))
+                    tiles.append([w[:, 4 * NB * s : 4 * NB * (s + 1)] for s in range(CH)])
             return tiles
 
-        w_i = load_gate(0)
-        w_f = load_gate(1)
+        load_scales(0, 3 * H)
+        w_i = load_gate(0, False)
+        w_f = load_gate(1, False)
+
+        slots = [(aux, "aux"), (aux, "aux"), (accp, "acc0"), (accp, "acc1"), (accp, "acc2"), (accp, "acc0"), (accp, "acc1"), (accp, "acc2")]
 
         grouped = keep.tile([P, PASSES * NB], BF16, align_bytes=64)
         codes = keep.tile([P, PASSES * P], U32, align_bytes=64)
@@ -78,9 +99,11 @@ def tile_layernormdropoutlstmcell_w_kernel(
         grouped_w = grouped[:].bitcast(F32).rearrange("p (c b u) -> p c b u", b=P, u=2)
         xw = x_sb[:].bitcast(F32)
         hw = hx_sb[:].bitcast(F32)
+        xts = []
         for h in range(4):
             n_c = 2 if h < 3 else 1
-            xt = aux.tile([P, NB], F32, tag="aux")
+            pool, tag = slots[h]
+            xt = pool.tile([P, NB], F32, tag=tag)
             for j in range(n_c):
                 c = 2 * h + j
                 src = xw if c < PASSES_X else hw
@@ -91,9 +114,13 @@ def tile_layernormdropoutlstmcell_w_kernel(
                         src[:, 256 * c0 + u : 256 * (c0 + 1) : 2],
                         ident_f[:],
                     )
-            nc.vector.tensor_copy(
+            xts.append(xt)
+        for h in range(4):
+            n_c = 2 if h < 3 else 1
+            eng_copy = nc.vector.tensor_copy if h % 2 == 0 else nc.scalar.copy
+            eng_copy(
                 out=grouped_w[:, 2 * h : 2 * h + n_c, :, :],
-                in_=xt[:, 0 : n_c * 256].rearrange("p (c u b) -> p c b u", u=2, b=P),
+                in_=xts[h][:, 0 : n_c * 256].rearrange("p (c u b) -> p c b u", u=2, b=P),
             )
         for lo, n in ((0, 2048), (2048, 1024), (3072, 512)):
             nc.vector.quantize_mx(
@@ -104,7 +131,8 @@ def tile_layernormdropoutlstmcell_w_kernel(
 
         gbb = keep.tile([P, 10 * H], BF16)
         for t in range(15):
-            bc = aux.tile([P, 2 * NB], BF16, tag="aux")
+            pool, tag = slots[(t + 4) % 8]
+            bc = pool.tile([P, 2 * NB], BF16, tag=tag)
             for e in range(2):
                 piece = 2 * t + e
                 row, s = piece // CH, piece % CH
@@ -115,7 +143,8 @@ def tile_layernormdropoutlstmcell_w_kernel(
                     start=True,
                     stop=True,
                 )
-            nc.scalar.copy(out=gbb[:, t * 2 * NB : (t + 1) * 2 * NB], in_=bc[:])
+            eng_copy = nc.scalar.copy if t % 2 == 0 else nc.vector.tensor_copy
+            eng_copy(out=gbb[:, t * 2 * NB : (t + 1) * 2 * NB], in_=bc[:])
 
         def gam(k, s):
             return gbb[:, 2 * k * H + s * NB : 2 * k * H + (s + 1) * NB]
@@ -137,17 +166,21 @@ def tile_layernormdropoutlstmcell_w_kernel(
                         out=acc[s][:],
                         lhsT=codes[:, P * c : P * (c + 1)].bitcast(FP8X4),
                         lhsT_scale=xs[:, P * c : P * (c + 1)],
-                        rhs=tiles[c][:, 4 * NB * s : 4 * NB * (s + 1)].bitcast(FP8X4),
+                        rhs=tiles[c][s].bitcast(FP8X4),
                         rhs_scale=plane[k:P, col0 : col0 + NB],
                         start=(c == 0),
                         stop=(c == PASSES - 1),
                     )
             return [a[:] for a in acc]
 
-        def ln_stats(chunks):
+        def new_stats():
             stats = small.tile([P, 6 * CH], F32, tag="stats")
-            for s in range(CH):
-                nc.vector.bn_stats(out=stats[:, 6 * s : 6 * s + 6], in_=chunks[s])
+            return stats
+
+        def bn(stats, chunks, s):
+            nc.vector.bn_stats(out=stats[:, 6 * s : 6 * s + 6], in_=chunks[s])
+
+        def finish_stats(stats):
             mv = small.tile([P, 2], F32, tag="mv")
             nc.vector.bn_aggr(out=mv[:], in_=stats[:])
             flt = small.tile([P, 1], F32, tag="flt")
@@ -162,13 +195,33 @@ def tile_layernormdropoutlstmcell_w_kernel(
             nc.gpsimd.tensor_tensor(out=rstd[:], in0=veps[:], in1=neg_half[:], op=ALU.pow)
             return mv[:, 0:1], rstd[:]
 
-        def ln_apply(dst, chunks, k, mean, rstd, s):
+        def centre(dst, chunks, k, mean, s):
             nc.vector.scalar_tensor_tensor(
                 out=dst[:, cols(s)], in0=chunks[s], scalar=mean, in1=gam(k, s), op0=ALU.subtract, op1=ALU.mult
             )
+
+        def rescale(dst, k, rstd, s):
             nc.vector.scalar_tensor_tensor(
                 out=dst[:, cols(s)], in0=dst[:, cols(s)], scalar=rstd, in1=bet(k, s), op0=ALU.mult, op1=ALU.add
             )
+
+        def act(dst, src, func, s, bias=0.0):
+            nc.scalar.activation(out=dst[:, cols(s)], in_=src[:, cols(s)], func=func, bias=bias)
+
+        def tt(dst, a, b, op, s):
+            nc.vector.tensor_tensor(out=dst[:, cols(s)], in0=a[:, cols(s)], in1=b[:, cols(s)], op=op)
+
+        def layer_norm(dst, chunks, k, stats, after):
+            mean, rstd = finish_stats(stats)
+            centre(dst, chunks, k, mean, 0)
+            centre(dst, chunks, k, mean, 1)
+            rescale(dst, k, rstd, 0)
+            after(0)
+            rescale(dst, k, rstd, 1)
+            after(1)
+            centre(dst, chunks, k, mean, 2)
+            rescale(dst, k, rstd, 2)
+            after(2)
 
         g_i = work.tile([P, H], F32)
         g_f = work.tile([P, H], F32)
@@ -178,40 +231,48 @@ def tile_layernormdropoutlstmcell_w_kernel(
         th = work.tile([P, H], F32)
 
         acc_i = gate_passes(0, w_i)
-        w_g = load_gate(2)
-        mean, rstd = ln_stats(acc_i)
+        w_g = load_gate(2, True)
+        st = new_stats()
         for s in range(CH):
-            ln_apply(g_i, acc_i, 0, mean, rstd, s)
-            nc.scalar.activation(out=g_i[:, cols(s)], in_=g_i[:, cols(s)], func=ACT.Sigmoid)
+            bn(st, acc_i, s)
+        layer_norm(g_i, acc_i, 0, st, lambda s: act(g_i, g_i, ACT.Sigmoid, s))
 
         acc_f = gate_passes(1, w_f)
-        w_o = load_gate(3)
-        mean, rstd = ln_stats(acc_f)
+        load_scales(3 * H, 4 * H)
+        w_o = load_gate(3, True)
+        st = new_stats()
         for s in range(CH):
-            ln_apply(g_f, acc_f, 1, mean, rstd, s)
-            nc.scalar.activation(out=g_f[:, cols(s)], in_=g_f[:, cols(s)], func=ACT.Sigmoid, bias=1.0)
-            nc.vector.tensor_tensor(out=g_f[:, cols(s)], in0=g_f[:, cols(s)], in1=cx_sb[:, cols(s)], op=ALU.mult)
+            bn(st, acc_f, s)
+        layer_norm(g_f, acc_f, 1, st, lambda s: act(g_f, g_f, ACT.Sigmoid, s, 1.0))
+        for s in range(CH):
+            tt(g_f, g_f, cx_sb, ALU.mult, s)
 
         acc_g = gate_passes(2, w_g)
-        mean, rstd = ln_stats(acc_g)
+        acc_o = gate_passes(3, w_o)
+        st = new_stats()
         for s in range(CH):
-            ln_apply(g_g, acc_g, 2, mean, rstd, s)
-            nc.scalar.activation(out=g_g[:, cols(s)], in_=g_g[:, cols(s)], func=ACT.Tanh)
-            nc.vector.tensor_tensor(out=g_g[:, cols(s)], in0=g_g[:, cols(s)], in1=g_i[:, cols(s)], op=ALU.mult)
-            nc.vector.tensor_tensor(out=g_g[:, cols(s)], in0=g_g[:, cols(s)], in1=g_f[:, cols(s)], op=ALU.add)
-
+            bn(st, acc_g, s)
+        layer_norm(g_g, acc_g, 2, st, lambda s: act(g_g, g_g, ACT.Tanh, s))
         c_chunks = [g_g[:, cols(s)] for s in range(CH)]
-        mean, rstd = ln_stats(c_chunks)
+        st = new_stats()
         for s in range(CH):
-            ln_apply(cy, c_chunks, 4, mean, rstd, s)
-            nc.scalar.activation(out=th[:, cols(s)], in_=cy[:, cols(s)], func=ACT.Tanh)
+            tt(g_g, g_g, g_i, ALU.mult, s)
+            tt(g_g, g_g, g_f, ALU.add, s)
+            bn(st, c_chunks, s)
+
+        layer_norm(cy, c_chunks, 4, st, lambda s: act(th, cy, ACT.Tanh, s))
         nc.sync.dma_start(out=out_2, in_=cy[:])
 
-        acc_o = gate_passes(3, w_o)
-        mean, rstd = ln_stats(acc_o)
+        st = new_stats()
         for s in range(CH):
-            ln_apply(g_o, acc_o, 3, mean, rstd, s)
-            nc.scalar.activation(out=g_o[:, cols(s)], in_=g_o[:, cols(s)], func=ACT.Sigmoid)
-            nc.vector.tensor_tensor(out=g_o[:, cols(s)], in0=g_o[:, cols(s)], in1=th[:, cols(s)], op=ALU.mult)
+            bn(st, acc_o, s)
+        mean, rstd = finish_stats(st)
+        for s in range(CH):
+            centre(g_o, acc_o, 3, mean, s)
+        for s in range(CH):
+            rescale(g_o, 3, rstd, s)
+            act(g_o, g_o, ACT.Sigmoid, s)
+        for s in range(CH):
+            tt(g_o, g_o, th, ALU.mult, s)
             nc.sync.dma_start(out=out_0[:, cols(s)], in_=g_o[:, cols(s)])
-            nc.sync.dma_start(out=out_1[:, cols(s)], in_=g_o[:, cols(s)])
+            nc.scalar.dma_start(out=out_1[:, cols(s)], in_=g_o[:, cols(s)])

@@ -69,9 +69,16 @@ def tile_layernormdropoutlstmcell_w_kernel(
                     in_=whh_s[:, 4 * q : 4 * q + 4, lo:hi].bitcast(I32),
                 )
 
-        def load_gate(gate, split_last):
+        def load_scale_piece(plane, rows, src, q, lo, hi):
+            nc.sync.dma_start(
+                out=plane[32 * q : 32 * q + rows, lo:hi].bitcast(I32), in_=src[:, 4 * q : 4 * q + 4, lo:hi].bitcast(I32)
+            )
+
+        def load_gate(gate, split_last, woven=()):
             tiles = []
             for c in range(PASSES):
+                for plane, rows, s_src, q in woven[2 * c : 2 * c + 2]:
+                    load_scale_piece(plane, rows, s_src, q, gate * H, (gate + 1) * H)
                 src = wih_w[c] if c < PASSES_X else whh_w[c - PASSES_X]
                 src = src.rearrange("p n t -> p (n t)")[:, gate * 4 * H : (gate + 1) * 4 * H]
                 if split_last and c == PASSES - 1:
@@ -238,8 +245,8 @@ def tile_layernormdropoutlstmcell_w_kernel(
         layer_norm(g_i, acc_i, 0, st, lambda s: act(g_i, g_i, ACT.Sigmoid, s))
 
         acc_f = gate_passes(1, w_f)
-        load_scales(3 * H, 4 * H)
-        w_o = load_gate(3, True)
+        woven_o = [(planes_ih, 16, wih_s, q) for q in (0, 2, 1, 3)] + [(planes_hh, 12, whh_s, q) for q in (0, 2, 1, 3)]
+        w_o = load_gate(3, True, woven_o)
         st = new_stats()
         for s in range(CH):
             bn(st, acc_f, s)
@@ -267,12 +274,29 @@ def tile_layernormdropoutlstmcell_w_kernel(
         for s in range(CH):
             bn(st, acc_o, s)
         mean, rstd = finish_stats(st)
-        for s in range(CH):
-            centre(g_o, acc_o, 3, mean, s)
-        for s in range(CH):
-            rescale(g_o, 3, rstd, s)
-            act(g_o, g_o, ACT.Sigmoid, s)
-        for s in range(CH):
-            tt(g_o, g_o, th, ALU.mult, s)
-            nc.sync.dma_start(out=out_0[:, cols(s)], in_=g_o[:, cols(s)])
-            nc.scalar.dma_start(out=out_1[:, cols(s)], in_=g_o[:, cols(s)])
+        shift, shift_op = mean, ALU.subtract
+        pieces = ((0, 512), (512, 1024), (1024, 1536))
+        for lo, hi in pieces:
+            b = lo // NB
+            nc.vector.scalar_tensor_tensor(
+                out=g_o[:, lo:hi],
+                in0=acc_o[b][:, lo - b * NB : hi - b * NB],
+                scalar=shift,
+                in1=gbb[:, 6 * H + lo : 6 * H + hi],
+                op0=shift_op,
+                op1=ALU.mult,
+            )
+        for lo, hi in pieces:
+            nc.vector.scalar_tensor_tensor(
+                out=g_o[:, lo:hi],
+                in0=g_o[:, lo:hi],
+                scalar=rstd,
+                in1=gbb[:, 7 * H + lo : 7 * H + hi],
+                op0=ALU.mult,
+                op1=ALU.add,
+            )
+            nc.scalar.activation(out=g_o[:, lo:hi], in_=g_o[:, lo:hi], func=ACT.Sigmoid)
+        for lo, hi in pieces:
+            nc.vector.tensor_tensor(out=g_o[:, lo:hi], in0=g_o[:, lo:hi], in1=th[:, lo:hi], op=ALU.mult)
+            nc.sync.dma_start(out=out_0[:, lo:hi], in_=g_o[:, lo:hi])
+            nc.scalar.dma_start(out=out_1[:, lo:hi], in_=g_o[:, lo:hi])

@@ -219,16 +219,25 @@ def tile_layernormdropoutlstmcell_w_kernel(
             nc.vector.tensor_tensor(out=dst[:, cols(s)], in0=a[:, cols(s)], in1=b[:, cols(s)], op=op)
 
         def layer_norm(dst, chunks, k, stats, after):
-            mean, rstd = finish_stats(stats)
+            mv = small.tile([P, 2], F32, tag="mv")
+            nc.vector.bn_aggr(out=mv[:], in_=stats[:])
+            mean = mv[:, 0:1]
+            flt = small.tile([P, 1], F32, tag="flt")
+            nc.vector.tensor_scalar(
+                out=flt[:], in0=mv[:, 1:2], scalar1=EPS, scalar2=0.01, op0=ALU.is_lt, op1=ALU.mult
+            )
             centre(dst, chunks, k, mean, 0)
+            veps = small.tile([P, 1], F32, tag="veps")
+            nc.vector.scalar_tensor_tensor(
+                out=veps[:], in0=mv[:, 1:2], scalar=EPS, in1=flt[:], op0=ALU.add, op1=ALU.add
+            )
+            rstd = small.tile([P, 1], F32, tag="rstd")
+            nc.gpsimd.tensor_tensor(out=rstd[:], in0=veps[:], in1=neg_half[:], op=ALU.pow)
             centre(dst, chunks, k, mean, 1)
-            rescale(dst, k, rstd, 0)
-            after(0)
-            rescale(dst, k, rstd, 1)
-            after(1)
             centre(dst, chunks, k, mean, 2)
-            rescale(dst, k, rstd, 2)
-            after(2)
+            for s in range(CH):
+                rescale(dst, k, rstd[:], s)
+                after(s)
 
         g_i = work.tile([P, H], F32)
         g_f = work.tile([P, H], F32)
@@ -262,10 +271,15 @@ def tile_layernormdropoutlstmcell_w_kernel(
         layer_norm(g_g, acc_g, 2, st, lambda s: act(g_g, g_g, ACT.Tanh, s))
         c_chunks = [g_g[:, cols(s)] for s in range(CH)]
         st = new_stats()
-        for s in range(CH):
-            tt(g_g, g_g, g_i, ALU.mult, s)
-            tt(g_g, g_g, g_f, ALU.add, s)
-            bn(st, c_chunks, s)
+        tt(g_g, g_g, g_i, ALU.mult, 0)
+        tt(g_g, g_g, g_i, ALU.mult, 1)
+        tt(g_g, g_g, g_f, ALU.add, 0)
+        tt(g_g, g_g, g_i, ALU.mult, 2)
+        tt(g_g, g_g, g_f, ALU.add, 1)
+        bn(st, c_chunks, 0)
+        tt(g_g, g_g, g_f, ALU.add, 2)
+        bn(st, c_chunks, 1)
+        bn(st, c_chunks, 2)
 
         layer_norm(cy, c_chunks, 4, st, lambda s: act(th, cy, ACT.Tanh, s))
         nc.sync.dma_start(out=out_2, in_=cy[:])
@@ -273,29 +287,8 @@ def tile_layernormdropoutlstmcell_w_kernel(
         st = new_stats()
         for s in range(CH):
             bn(st, acc_o, s)
-        mean, rstd = finish_stats(st)
-        shift, shift_op = mean, ALU.subtract
+        layer_norm(g_o, acc_o, 3, st, lambda s: act(g_o, g_o, ACT.Sigmoid, s))
         pieces = ((0, 512), (512, 1024), (1024, 1536))
-        for lo, hi in pieces:
-            b = lo // NB
-            nc.vector.scalar_tensor_tensor(
-                out=g_o[:, lo:hi],
-                in0=acc_o[b][:, lo - b * NB : hi - b * NB],
-                scalar=shift,
-                in1=gbb[:, 6 * H + lo : 6 * H + hi],
-                op0=shift_op,
-                op1=ALU.mult,
-            )
-        for lo, hi in pieces:
-            nc.vector.scalar_tensor_tensor(
-                out=g_o[:, lo:hi],
-                in0=g_o[:, lo:hi],
-                scalar=rstd,
-                in1=gbb[:, 7 * H + lo : 7 * H + hi],
-                op0=ALU.mult,
-                op1=ALU.add,
-            )
-            nc.scalar.activation(out=g_o[:, lo:hi], in_=g_o[:, lo:hi], func=ACT.Sigmoid)
         for lo, hi in pieces:
             nc.vector.tensor_tensor(out=g_o[:, lo:hi], in0=g_o[:, lo:hi], in1=th[:, lo:hi], op=ALU.mult)
             nc.sync.dma_start(out=out_0[:, lo:hi], in_=g_o[:, lo:hi])

@@ -34,7 +34,7 @@ def tile_layernormdropoutlstmcell_w_kernel(
         work = stack.enter_context(tc.tile_pool(name="work", bufs=1))
         small = stack.enter_context(tc.tile_pool(name="small", bufs=3))
         accp = stack.enter_context(tc.psum_pool(name="accp", bufs=2))
-        aux = stack.enter_context(tc.psum_pool(name="aux", bufs=2))
+        aux = stack.enter_context(tc.psum_pool(name="aux", bufs=1))
 
         planes_ih = keep.tile([P, 4 * H], U8, align_bytes=64)
         planes_hh = keep.tile([P, 4 * H], U8, align_bytes=64)
@@ -98,7 +98,7 @@ def tile_layernormdropoutlstmcell_w_kernel(
         w_i = load_gate(0, False)
         w_f = load_gate(1, False)
 
-        slots = [(aux, "aux"), (aux, "aux"), (accp, "acc0"), (accp, "acc1"), (accp, "acc2"), (accp, "acc0"), (accp, "acc1"), (accp, "acc2")]
+        slots = [(accp, "acc0"), (accp, "acc1"), (accp, "acc2"), (accp, "acc0"), (accp, "acc1"), (accp, "acc2")]
 
         grouped = keep.tile([P, PASSES * NB], BF16, align_bytes=64)
         codes = keep.tile([P, PASSES * P], U32, align_bytes=64)
@@ -137,23 +137,35 @@ def tile_layernormdropoutlstmcell_w_kernel(
             )
 
         gbb = keep.tile([P, 10 * H], BF16)
-        for t in range(15):
-            pool, tag = slots[(t + 4) % 8]
-            bc = pool.tile([P, 2 * NB], BF16, tag=tag)
-            for e in range(2):
-                piece = 2 * t + e
+
+        def spread(dst, pieces):
+            for e, piece in enumerate(pieces):
                 row, s = piece // CH, piece % CH
                 nc.tensor.matmul(
-                    out=bc[:, e * NB : (e + 1) * NB],
+                    out=dst[:, e * NB : (e + 1) * NB],
                     lhsT=ident_b[:, row : row + 1].to_broadcast([P, P]),
                     rhs=gb[:, s * NB : (s + 1) * NB],
                     start=True,
                     stop=True,
                 )
+
+        groups = [(2 * t, 2 * t + 1) for t in range(12)] + [(27, 28), (29,)]
+        for t, pieces in enumerate(groups):
+            pool, tag = slots[(t + 4) % 6]
+            bc = pool.tile([P, 2 * NB], BF16, tag=tag)
+            spread(bc, pieces)
             eng_copy = nc.scalar.copy if t % 2 == 0 else nc.vector.tensor_copy
-            eng_copy(out=gbb[:, t * 2 * NB : (t + 1) * 2 * NB], in_=bc[:])
+            eng_copy(
+                out=gbb[:, pieces[0] * NB : (pieces[0] + len(pieces)) * NB], in_=bc[:, 0 : len(pieces) * NB]
+            )
+        g4a = aux.tile([P, 2 * NB], BF16, tag="g4a")
+        spread(g4a, (24, 25))
+        g4b = aux.tile([P, NB], BF16, tag="g4b")
+        spread(g4b, (26,))
 
         def gam(k, s):
+            if k == 4:
+                return g4a[:, s * NB : (s + 1) * NB] if s < 2 else g4b[:]
             return gbb[:, 2 * k * H + s * NB : 2 * k * H + (s + 1) * NB]
 
         def bet(k, s):

@@ -29,7 +29,8 @@ def tile_layernormdropoutlstmcell_w_kernel(
     nc = tc.nc
     with ExitStack() as stack:
         keep = stack.enter_context(tc.tile_pool(name="keep", bufs=1))
-        wpool = stack.enter_context(tc.tile_pool(name="wpool", bufs=18))
+        wpair = stack.enter_context(tc.tile_pool(name="wpair", bufs=4))
+        wpool = stack.enter_context(tc.tile_pool(name="wpool", bufs=12))
         wlast = stack.enter_context(tc.tile_pool(name="wlast", bufs=6))
         work = stack.enter_context(tc.tile_pool(name="work", bufs=1))
         small = stack.enter_context(tc.tile_pool(name="small", bufs=3))
@@ -74,9 +75,9 @@ def tile_layernormdropoutlstmcell_w_kernel(
                 out=plane[32 * q : 32 * q + rows, lo:hi].bitcast(I32), in_=src[:, 4 * q : 4 * q + 4, lo:hi].bitcast(I32)
             )
 
-        def load_gate(gate, split_last, woven=()):
+        def load_gate(gate, split_last, woven=(), first=0):
             tiles = []
-            for c in range(PASSES):
+            for c in range(first, PASSES):
                 for plane, rows, s_src, q in woven[2 * c : 2 * c + 2]:
                     load_scale_piece(plane, rows, s_src, q, gate * H, (gate + 1) * H)
                 src = wih_w[c] if c < PASSES_X else whh_w[c - PASSES_X]
@@ -95,8 +96,15 @@ def tile_layernormdropoutlstmcell_w_kernel(
             return tiles
 
         load_scales(0, 3 * H)
-        w_i = load_gate(0, False)
-        w_f = load_gate(1, False)
+        w_i, w_f = [], []
+        for c in range(PASSES_X):
+            pair = wpair.tile([P, 8 * H], U8, tag="pair", align_bytes=64)
+            src = wih_w[c].rearrange("p n t -> p (n t)")[:, 0 : 8 * H]
+            nc.sync.dma_start(out=pair[:].bitcast(I32), in_=src.bitcast(I32))
+            for gate, tiles in ((0, w_i), (1, w_f)):
+                tiles.append([pair[:, 4 * (gate * H + NB * s) : 4 * (gate * H + NB * (s + 1))] for s in range(CH)])
+        w_i += load_gate(0, False, first=PASSES_X)
+        w_f += load_gate(1, False, first=PASSES_X)
 
         slots = [(accp, "acc0"), (accp, "acc1"), (accp, "acc2"), (accp, "acc0"), (accp, "acc1"), (accp, "acc2")]
 

from contextlib import ExitStack

import concourse.mybir as mybir
from concourse.masks import make_identity

F32 = mybir.dt.float32
BF16 = mybir.dt.bfloat16
I32 = mybir.dt.int32
U8 = mybir.dt.uint8
U32 = mybir.dt.uint32
FP8X4 = mybir.dt.float8_e4m3fn_x4
ALU = mybir.AluOpType
ACT = mybir.ActivationFunctionType

P = 128
IN = 2048
H = 1536
PASSES_X = 4
PASSES = 7
NB = 512
CH = 3
EPS = 1e-12
FLOPS = 2 * 128 * (2048 + 1536) * 4 * 1536


def tile_layernormdropoutlstmcell_w_kernel(
    tc, x, hx, cx, wih_w, wih_s, whh_w, whh_s, gamma, beta, out_0, out_1, out_2
):
    nc = tc.nc
    with ExitStack() as stack:
        keep = stack.enter_context(tc.tile_pool(name="keep", bufs=1))
        wpair = stack.enter_context(tc.tile_pool(name="wpair", bufs=4))
        wpool = stack.enter_context(tc.tile_pool(name="wpool", bufs=12))
        wlast = stack.enter_context(tc.tile_pool(name="wlast", bufs=6))
        work = stack.enter_context(tc.tile_pool(name="work", bufs=1))
        small = stack.enter_context(tc.tile_pool(name="small", bufs=3))
        accp = stack.enter_context(tc.psum_pool(name="accp", bufs=2))
        aux = stack.enter_context(tc.psum_pool(name="aux", bufs=1))

        planes_ih = keep.tile([P, 4 * H], U8, align_bytes=64)
        planes_hh = keep.tile([P, 4 * H], U8, align_bytes=64)
        gb = keep.tile([P, H], BF16)
        nc.vector.memset(gb[:].bitcast(I32), 0)
        nc.vector.memset(planes_ih[:].bitcast(I32), 0)
        nc.vector.memset(planes_hh[:].bitcast(I32), 0)
        neg_half = keep.tile([P, 1], F32)
        nc.vector.memset(neg_half[:], -0.5)
        ident_f = keep.tile([P, P], F32)
        make_identity(nc, ident_f[:])
        ident_b = keep.tile([P, P], BF16)
        make_identity(nc, ident_b[:])

        x_sb = keep.tile([P, IN], BF16)
        hx_sb = keep.tile([P, H], BF16)
        cx_sb = keep.tile([P, H], BF16)
        nc.sync.dma_start(out=x_sb[:], in_=x)
        nc.sync.dma_start(out=hx_sb[:], in_=hx)
        nc.scalar.dma_start(out=gb[0:10:2, :], in_=gamma)
        nc.scalar.dma_start(out=gb[1:10:2, :], in_=beta)
        nc.scalar.dma_start(out=cx_sb[:], in_=cx)

        def load_scales(lo, hi):
            for q in (0, 2, 1, 3):
                nc.sync.dma_start(
                    out=planes_ih[32 * q : 32 * q + 16, lo:hi].bitcast(I32),
                    in_=wih_s[:, 4 * q : 4 * q + 4, lo:hi].bitcast(I32),
                )
                nc.sync.dma_start(
                    out=planes_hh[32 * q : 32 * q + 12, lo:hi].bitcast(I32),
                    in_=whh_s[:, 4 * q : 4 * q + 4, lo:hi].bitcast(I32),
                )

        def load_scale_piece(plane, rows, src, q, lo, hi):
            nc.sync.dma_start(
                out=plane[32 * q : 32 * q + rows, lo:hi].bitcast(I32), in_=src[:, 4 * q : 4 * q + 4, lo:hi].bitcast(I32)
            )

        def load_gate(gate, split_last, woven=(), first=0):
            tiles = []
            for c in range(first, PASSES):
                for plane, rows, s_src, q in woven[2 * c : 2 * c + 2]:
                    load_scale_piece(plane, rows, s_src, q, gate * H, (gate + 1) * H)
                src = wih_w[c] if c < PASSES_X else whh_w[c - PASSES_X]
                src = src.rearrange("p n t -> p (n t)")[:, gate * 4 * H : (gate + 1) * 4 * H]
                if split_last and c == PASSES - 1:
                    pieces = []
                    for s in range(CH):
                        wl = wlast.tile([P, 4 * NB], U8, tag="wl", align_bytes=64)
                        nc.sync.dma_start(out=wl[:].bitcast(I32), in_=src[:, 4 * NB * s : 4 * NB * (s + 1)].bitcast(I32))
                        pieces.append(wl[:])
                    tiles.append(pieces)
                else:
                    w = wpool.tile([P, 4 * H], U8, tag="w", align_bytes=64)
                    nc.sync.dma_start(out=w[:].bitcast(I32), in_=src.bitcast(I32))
                    tiles.append([w[:, 4 * NB * s : 4 * NB * (s + 1)] for s in range(CH)])
            return tiles

        load_scales(0, 3 * H)
        w_i, w_f = [], []
        for c in range(PASSES_X):
            pair = wpair.tile([P, 8 * H], U8, tag="pair", align_bytes=64)
            src = wih_w[c].rearrange("p n t -> p (n t)")[:, 0 : 8 * H]
            nc.sync.dma_start(out=pair[:].bitcast(I32), in_=src.bitcast(I32))
            for gate, tiles in ((0, w_i), (1, w_f)):
                tiles.append([pair[:, 4 * (gate * H + NB * s) : 4 * (gate * H + NB * (s + 1))] for s in range(CH)])
        w_i += load_gate(0, False, first=PASSES_X)
        w_f += load_gate(1, False, first=PASSES_X)

        slots = [(accp, "acc0"), (accp, "acc1"), (accp, "acc2"), (accp, "acc0"), (accp, "acc1"), (accp, "acc2")]

        grouped = keep.tile([P, PASSES * NB], BF16, align_bytes=64)
        codes = keep.tile([P, PASSES * P], U32, align_bytes=64)
        xs = keep.tile([P, PASSES * P], U8, align_bytes=64)
        grouped_w = grouped[:].bitcast(F32).rearrange("p (c b u) -> p c b u", b=P, u=2)
        xw = x_sb[:].bitcast(F32)
        hw = hx_sb[:].bitcast(F32)
        xts = []
        for h in range(4):
            n_c = 2 if h < 3 else 1
            pool, tag = slots[h]
            xt = pool.tile([P, NB], F32, tag=tag)
            for j in range(n_c):
                c = 2 * h + j
                src = xw if c < PASSES_X else hw
                c0 = c if c < PASSES_X else c - PASSES_X
                for u in range(2):
                    nc.tensor.transpose(
                        xt[:, (2 * j + u) * P : (2 * j + u + 1) * P],
                        src[:, 256 * c0 + u : 256 * (c0 + 1) : 2],
                        ident_f[:],
                    )
            xts.append(xt)
        for h in range(4):
            n_c = 2 if h < 3 else 1
            eng_copy = nc.vector.tensor_copy if h % 2 == 0 else nc.scalar.copy
            eng_copy(
                out=grouped_w[:, 2 * h : 2 * h + n_c, :, :],
                in_=xts[h][:, 0 : n_c * 256].rearrange("p (c u b) -> p c b u", u=2, b=P),
            )
        for lo, n in ((0, 2048), (2048, 1024), (3072, 512)):
            nc.vector.quantize_mx(
                out=codes[:, lo // 4 : (lo + n) // 4].bitcast(FP8X4),
                scales=xs[:, lo // 4 : (lo + n) // 4],
                in_=grouped[:, lo : lo + n],
            )

        gbb = keep.tile([P, 10 * H], BF16)

        def spread(dst, pieces):
            for e, piece in enumerate(pieces):
                row, s = piece // CH, piece % CH
                nc.tensor.matmul(
                    out=dst[:, e * NB : (e + 1) * NB],
                    lhsT=ident_b[:, row : row + 1].to_broadcast([P, P]),
                    rhs=gb[:, s * NB : (s + 1) * NB],
                    start=True,
                    stop=True,
                )

        groups = [(2 * t, 2 * t + 1) for t in range(12)] + [(27, 28), (29,)]
        for t, pieces in enumerate(groups):
            pool, tag = slots[(t + 4) % 6]
            bc = pool.tile([P, 2 * NB], BF16, tag=tag)
            spread(bc, pieces)
            eng_copy = nc.scalar.copy if t % 2 == 0 else nc.vector.tensor_copy
            eng_copy(
                out=gbb[:, pieces[0] * NB : (pieces[0] + len(pieces)) * NB], in_=bc[:, 0 : len(pieces) * NB]
            )
        g4a = aux.tile([P, 2 * NB], BF16, tag="g4a")
        spread(g4a, (24, 25))
        g4b = aux.tile([P, NB], BF16, tag="g4b")
        spread(g4b, (26,))

        def gam(k, s):
            if k == 4:
                return g4a[:, s * NB : (s + 1) * NB] if s < 2 else g4b[:]
            return gbb[:, 2 * k * H + s * NB : 2 * k * H + (s + 1) * NB]

        def bet(k, s):
            return gbb[:, (2 * k + 1) * H + s * NB : (2 * k + 1) * H + (s + 1) * NB]

        def cols(s):
            return slice(s * NB, (s + 1) * NB)

        def gate_passes(gate, tiles):
            acc = [accp.tile([P, NB], F32, name="acc%d" % s, tag="acc%d" % s) for s in range(CH)]
            for c in range(PASSES):
                plane = planes_ih if c < PASSES_X else planes_hh
                k = 4 * c if c < PASSES_X else 4 * (c - PASSES_X)
                for s in range(CH):
                    col0 = gate * H + s * NB
                    nc.tensor.matmul_mx(
                        out=acc[s][:],
                        lhsT=codes[:, P * c : P * (c + 1)].bitcast(FP8X4),
                        lhsT_scale=xs[:, P * c : P * (c + 1)],
                        rhs=tiles[c][s].bitcast(FP8X4),
                        rhs_scale=plane[k:P, col0 : col0 + NB],
                        start=(c == 0),
                        stop=(c == PASSES - 1),
                    )
            return [a[:] for a in acc]

        def new_stats():
            stats = small.tile([P, 6 * CH], F32, tag="stats")
            return stats

        def bn(stats, chunks, s):
            nc.vector.bn_stats(out=stats[:, 6 * s : 6 * s + 6], in_=chunks[s])

        def finish_stats(stats):
            mv = small.tile([P, 2], F32, tag="mv")
            nc.vector.bn_aggr(out=mv[:], in_=stats[:])
            flt = small.tile([P, 1], F32, tag="flt")
            nc.vector.tensor_scalar(
                out=flt[:], in0=mv[:, 1:2], scalar1=EPS, scalar2=0.01, op0=ALU.is_lt, op1=ALU.mult
            )
            veps = small.tile([P, 1], F32, tag="veps")
            nc.vector.scalar_tensor_tensor(
                out=veps[:], in0=mv[:, 1:2], scalar=EPS, in1=flt[:], op0=ALU.add, op1=ALU.add
            )
            rstd = small.tile([P, 1], F32, tag="rstd")
            nc.gpsimd.tensor_tensor(out=rstd[:], in0=veps[:], in1=neg_half[:], op=ALU.pow)
            return mv[:, 0:1], rstd[:]

        def centre(dst, chunks, k, mean, s):
            nc.vector.scalar_tensor_tensor(
                out=dst[:, cols(s)], in0=chunks[s], scalar=mean, in1=gam(k, s), op0=ALU.subtract, op1=ALU.mult
            )

        def rescale(dst, k, rstd, s):
            nc.vector.scalar_tensor_tensor(
                out=dst[:, cols(s)], in0=dst[:, cols(s)], scalar=rstd, in1=bet(k, s), op0=ALU.mult, op1=ALU.add
            )

        def act(dst, src, func, s, bias=0.0):
            nc.scalar.activation(out=dst[:, cols(s)], in_=src[:, cols(s)], func=func, bias=bias)

        def tt(dst, a, b, op, s):
            nc.vector.tensor_tensor(out=dst[:, cols(s)], in0=a[:, cols(s)], in1=b[:, cols(s)], op=op)

        def layer_norm(dst, chunks, k, stats, after):
            mv = small.tile([P, 2], F32, tag="mv")
            nc.vector.bn_aggr(out=mv[:], in_=stats[:])
            mean = mv[:, 0:1]
            flt = small.tile([P, 1], F32, tag="flt")
            nc.vector.tensor_scalar(
                out=flt[:], in0=mv[:, 1:2], scalar1=EPS, scalar2=0.01, op0=ALU.is_lt, op1=ALU.mult
            )
            centre(dst, chunks, k, mean, 0)
            veps = small.tile([P, 1], F32, tag="veps")
            nc.vector.scalar_tensor_tensor(
                out=veps[:], in0=mv[:, 1:2], scalar=EPS, in1=flt[:], op0=ALU.add, op1=ALU.add
            )
            rstd = small.tile([P, 1], F32, tag="rstd")
            nc.gpsimd.tensor_tensor(out=rstd[:], in0=veps[:], in1=neg_half[:], op=ALU.pow)
            centre(dst, chunks, k, mean, 1)
            centre(dst, chunks, k, mean, 2)
            for s in range(CH):
                rescale(dst, k, rstd[:], s)
                after(s)

        g_i = work.tile([P, H], F32)
        g_f = work.tile([P, H], F32)
        g_g = work.tile([P, H], F32)
        g_o = work.tile([P, H], F32)
        cy = work.tile([P, H], F32)
        th = work.tile([P, H], F32)

        acc_i = gate_passes(0, w_i)
        w_g = load_gate(2, True)
        st = new_stats()
        for s in range(CH):
            bn(st, acc_i, s)
        layer_norm(g_i, acc_i, 0, st, lambda s: act(g_i, g_i, ACT.Sigmoid, s))

        acc_f = gate_passes(1, w_f)
        woven_o = [(planes_ih, 16, wih_s, q) for q in (0, 2, 1, 3)] + [(planes_hh, 12, whh_s, q) for q in (0, 2, 1, 3)]
        w_o = load_gate(3, True, woven_o)
        st = new_stats()
        for s in range(CH):
            bn(st, acc_f, s)
        layer_norm(g_f, acc_f, 1, st, lambda s: act(g_f, g_f, ACT.Sigmoid, s, 1.0))
        for s in range(CH):
            tt(g_f, g_f, cx_sb, ALU.mult, s)

        acc_g = gate_passes(2, w_g)
        acc_o = gate_passes(3, w_o)
        st = new_stats()
        for s in range(CH):
            bn(st, acc_g, s)
        layer_norm(g_g, acc_g, 2, st, lambda s: act(g_g, g_g, ACT.Tanh, s))
        c_chunks = [g_g[:, cols(s)] for s in range(CH)]
        st = new_stats()
        tt(g_g, g_g, g_i, ALU.mult, 0)
        tt(g_g, g_g, g_i, ALU.mult, 1)
        tt(g_g, g_g, g_f, ALU.add, 0)
        tt(g_g, g_g, g_i, ALU.mult, 2)
        tt(g_g, g_g, g_f, ALU.add, 1)
        bn(st, c_chunks, 0)
        tt(g_g, g_g, g_f, ALU.add, 2)
        bn(st, c_chunks, 1)
        bn(st, c_chunks, 2)

        layer_norm(cy, c_chunks, 4, st, lambda s: act(th, cy, ACT.Tanh, s))
        nc.sync.dma_start(out=out_2, in_=cy[:])

        st = new_stats()
        for s in range(CH):
            bn(st, acc_o, s)
        layer_norm(g_o, acc_o, 3, st, lambda s: act(g_o, g_o, ACT.Sigmoid, s))
        pieces = ((0, 512), (512, 1024), (1024, 1536))
        for lo, hi in pieces:
            nc.vector.tensor_tensor(out=g_o[:, lo:hi], in0=g_o[:, lo:hi], in1=th[:, lo:hi], op=ALU.mult)
            nc.sync.dma_start(out=out_0[:, lo:hi], in_=g_o[:, lo:hi])
            nc.scalar.dma_start(out=out_1[:, lo:hi], in_=g_o[:, lo:hi])
